import numpy as np
import ml_dtypes

BF16 = ml_dtypes.bfloat16


def bf(x):
    return np.asarray(x, np.float32).astype(BF16)


def f32(x):
    return np.asarray(x, np.float32)


def f64(x):
    return np.asarray(x).astype(np.float64)


def striped(idx):
    return np.tile(idx.reshape(-1, 16).T, (8, 1))


D, S, F, M, N = 128, 4096, 128, 256, 2048
ALPHA = 1.702
LIMIT = 7.0


def setup_inputs():
    return {"x": bf(np.random.standard_normal((D, S))), "w1": bf(3.0 * np.random.standard_normal((D, M)) / np.sqrt(D)), "b1": f32(0.3 * np.random.standard_normal((M, 1))), "w2": bf(0.25 * np.random.standard_normal((F, D)) / np.sqrt(F)), "b2": f32(0.2 * np.random.standard_normal((D, 1))), "ew": f32(0.1 + 0.9 * np.random.random_sample((1, N))), "offs": striped(np.random.permutation(S)[:N])}


def reference(x, w1, b1, w2, b2, ew, offs):
    idx = offs[:16].T.reshape(-1)
    t = f64(w1).T @ f64(x)[:, idx] + f64(b1)
    glu = np.minimum(t[:F], LIMIT)
    lin = np.maximum(np.minimum(t[F:], LIMIT), -LIMIT)
    h = glu / (1.0 + np.exp(-ALPHA * glu)) * (lin + 1.0)
    return (f64(w2).T @ h + f64(b2)) * f64(ew)

@@ -1,0 +1,77 @@
+import concourse.mybir as mybir
+
+P = 128
+TOKENS = 4096
+ROUTED = 2048
+PIECE = 512
+PIECES = ROUTED // PIECE
+OFFSET_COLUMNS = PIECE // 16
+ALPHA = 1.702
+LIMIT = 7.0
+
+FLOPS = 2 * P * (2 * P) * ROUTED + 2 * P * P * ROUTED
+
+BF16, F32, U16 = mybir.dt.bfloat16, mybir.dt.float32, mybir.dt.uint16
+ADD, MULT = mybir.AluOpType.add, mybir.AluOpType.mult
+MIN, MAX = mybir.AluOpType.min, mybir.AluOpType.max
+SIGMOID = mybir.ActivationFunctionType.Sigmoid
+
+
+def tile_moemlpfused_kernel(tc, x, w1, b1, w2, b2, ew, offs, out):
+    nc = tc.nc
+    with (
+        tc.tile_pool(name="held", bufs=1) as held,
+        tc.tile_pool(name="work", bufs=2) as work,
+        tc.psum_pool(name="psum", bufs=2) as psum,
+    ):
+        offsets = held.tile([P, ROUTED // 16], U16, name="offsets")
+        tokens = held.tile([P, TOKENS], BF16, name="tokens")
+        w1_sb = held.tile([P, 2 * P], BF16, name="w1_sb")
+        w2_sb = held.tile([P, P], BF16, name="w2_sb")
+        b1_gate = held.tile([P, 1], F32, name="b1_gate")
+        b1_lin = held.tile([P, 1], F32, name="b1_lin")
+        b2_sb = held.tile([P, 1], F32, name="b2_sb")
+        routing = held.tile([P, ROUTED], F32, name="routing")
+
+        nc.sync.dma_start(offsets[:], offs)
+        nc.sync.dma_start(tokens[:], x)
+        nc.sync.dma_start(routing[:], ew.broadcast_to([P, ROUTED]))
+        nc.scalar.dma_start(w1_sb[:], w1)
+        nc.scalar.dma_start(b1_gate[:], b1[0:P, :])
+        nc.scalar.dma_start(b1_lin[:], b1[P : 2 * P, :])
+        nc.scalar.dma_start(w2_sb[:], w2)
+        nc.scalar.dma_start(b2_sb[:], b2)
+
+        for piece in range(PIECES):
+            columns = slice(piece * PIECE, (piece + 1) * PIECE)
+            picked = tokens[:].indirect(
+                offsets[:, piece * OFFSET_COLUMNS : (piece + 1) * OFFSET_COLUMNS]
+            )
+
+            t_gate = psum.tile([P, PIECE], F32, name="t_gate")
+            t_lin = psum.tile([P, PIECE], F32, name="t_lin")
+            nc.tensor.matmul(t_gate[:], w1_sb[:, 0:P], picked)
+            nc.tensor.matmul(t_lin[:], w1_sb[:, P : 2 * P], picked)
+
+            glu = work.tile([P, PIECE], F32, name="glu")
+            nc.vector.tensor_scalar(glu[:], t_gate[:], b1_gate[:], LIMIT, ADD, MIN)
+            sig = work.tile([P, PIECE], F32, name="sig")
+            nc.scalar.activation(sig[:], glu[:], SIGMOID, scale=ALPHA)
+
+            lin = work.tile([P, PIECE], F32, name="lin")
+            nc.vector.tensor_scalar(lin[:], t_lin[:], b1_lin[:], LIMIT, ADD, MIN)
+            lin1 = work.tile([P, PIECE], F32, name="lin1")
+            nc.vector.tensor_scalar(lin1[:], lin[:], -LIMIT, 1.0, MAX, ADD)
+
+            swish = work.tile([P, PIECE], F32, name="swish")
+            nc.vector.tensor_tensor(swish[:], glu[:], sig[:], MULT)
+            h = work.tile([P, PIECE], BF16, name="h")
+            nc.vector.tensor_tensor(h[:], swish[:], lin1[:], MULT)
+
+            y = psum.tile([P, PIECE], F32, name="y")
+            nc.tensor.matmul(y[:], w2_sb[:], h[:])
+            scaled = work.tile([P, PIECE], F32, name="scaled")
+            nc.vector.scalar_tensor_tensor(
+                scaled[:], y[:], b2_sb[:], routing[:, columns], ADD, MULT
+            )
+            nc.sync.dma_start(out[:, columns], scaled[:])

@@ -6,7 +6,7 @@ ROUTED = 2048
 PIECE = 512
 PIECES = ROUTED // PIECE
 OFFSET_COLUMNS = PIECE // 16
-ALPHA = 1.702
+PSUM_BANKS = 8
 LIMIT = 7.0
 
 FLOPS = 2 * P * (2 * P) * ROUTED + 2 * P * P * ROUTED
@@ -14,15 +14,16 @@ FLOPS = 2 * P * (2 * P) * ROUTED + 2 * P * P * ROUTED
 BF16, F32, U16 = mybir.dt.bfloat16, mybir.dt.float32, mybir.dt.uint16
 ADD, MULT = mybir.AluOpType.add, mybir.AluOpType.mult
 MIN, MAX = mybir.AluOpType.min, mybir.AluOpType.max
-SIGMOID = mybir.ActivationFunctionType.Sigmoid
+SWISH = mybir.ActivationFunctionType.Gelu_apprx_sigmoid
+IDENTITY = mybir.ActivationFunctionType.Identity
 
 
 def tile_moemlpfused_kernel(tc, x, w1, b1, w2, b2, ew, offs, out):
     nc = tc.nc
     with (
         tc.tile_pool(name="held", bufs=1) as held,
-        tc.tile_pool(name="work", bufs=2) as work,
-        tc.psum_pool(name="psum", bufs=2) as psum,
+        tc.tile_pool(name="work", bufs=PIECES) as work,
+        tc.psum_pool(name="psum", bufs=PSUM_BANKS) as psum,
     ):
         offsets = held.tile([P, ROUTED // 16], U16, name="offsets")
         tokens = held.tile([P, TOKENS], BF16, name="tokens")
@@ -30,46 +31,56 @@ def tile_moemlpfused_kernel(tc, x, w1, b1, w2, b2, ew, offs, out):
         w2_sb = held.tile([P, P], BF16, name="w2_sb")
         b1_gate = held.tile([P, 1], F32, name="b1_gate")
         b1_lin = held.tile([P, 1], F32, name="b1_lin")
+        b1_lin1 = held.tile([P, 1], F32, name="b1_lin1")
         b2_sb = held.tile([P, 1], F32, name="b2_sb")
         routing = held.tile([P, ROUTED], F32, name="routing")
+        limit = held.tile([P, 1], F32, name="limit")
+        swish_cap = held.tile([P, 1], F32, name="swish_cap")
 
         nc.sync.dma_start(offsets[:], offs)
-        nc.sync.dma_start(tokens[:], x)
-        nc.sync.dma_start(routing[:], ew.broadcast_to([P, ROUTED]))
-        nc.scalar.dma_start(w1_sb[:], w1)
-        nc.scalar.dma_start(b1_gate[:], b1[0:P, :])
-        nc.scalar.dma_start(b1_lin[:], b1[P : 2 * P, :])
-        nc.scalar.dma_start(w2_sb[:], w2)
-        nc.scalar.dma_start(b2_sb[:], b2)
+        nc.scalar.dma_start(tokens[:], x)
+        nc.gpsimd.dma_start(w1_sb[:], w1)
+        nc.sync.dma_start(b1_gate[:], b1[0:P, :])
+        nc.gpsimd.dma_start(b1_lin[:], b1[P : 2 * P, :])
+        nc.scalar.dma_start(routing[:], ew.broadcast_to([P, ROUTED]))
+        nc.gpsimd.dma_start(w2_sb[:], w2)
+        nc.sync.dma_start(b2_sb[:], b2)
 
+        nc.vector.memset(limit[:], LIMIT)
+        nc.scalar.activation(swish_cap[:], limit[:], SWISH)
+
+        nc.vector.tensor_scalar_add(b1_lin1[:], b1_lin[:], 1.0)
+
+        t_gate, t_lin = [], []
         for piece in range(PIECES):
-            columns = slice(piece * PIECE, (piece + 1) * PIECE)
             picked = tokens[:].indirect(
                 offsets[:, piece * OFFSET_COLUMNS : (piece + 1) * OFFSET_COLUMNS]
             )
+            t_gate.append(psum.tile([P, PIECE], F32, name=f"t_gate{piece}", tag="bank"))
+            t_lin.append(psum.tile([P, PIECE], F32, name=f"t_lin{piece}", tag="bank"))
+            nc.tensor.matmul(t_gate[piece][:], w1_sb[:, 0:P], picked)
+            nc.tensor.matmul(t_lin[piece][:], w1_sb[:, P : 2 * P], picked)
 
-            t_gate = psum.tile([P, PIECE], F32, name="t_gate")
-            t_lin = psum.tile([P, PIECE], F32, name="t_lin")
-            nc.tensor.matmul(t_gate[:], w1_sb[:, 0:P], picked)
-            nc.tensor.matmul(t_lin[:], w1_sb[:, P : 2 * P], picked)
-
-            glu = work.tile([P, PIECE], F32, name="glu")
-            nc.vector.tensor_scalar(glu[:], t_gate[:], b1_gate[:], LIMIT, ADD, MIN)
-            sig = work.tile([P, PIECE], F32, name="sig")
-            nc.scalar.activation(sig[:], glu[:], SIGMOID, scale=ALPHA)
-
-            lin = work.tile([P, PIECE], F32, name="lin")
-            nc.vector.tensor_scalar(lin[:], t_lin[:], b1_lin[:], LIMIT, ADD, MIN)
-            lin1 = work.tile([P, PIECE], F32, name="lin1")
-            nc.vector.tensor_scalar(lin1[:], lin[:], -LIMIT, 1.0, MAX, ADD)
-
+        h = []
+        for piece in range(PIECES):
             swish = work.tile([P, PIECE], F32, name="swish")
-            nc.vector.tensor_tensor(swish[:], glu[:], sig[:], MULT)
-            h = work.tile([P, PIECE], BF16, name="h")
-            nc.vector.tensor_tensor(h[:], swish[:], lin1[:], MULT)
+            nc.scalar.activation(swish[:], t_gate[piece][:], SWISH, bias=b1_gate[:])
+            lin_raw = work.tile([P, PIECE], F32, name="lin_raw")
+            nc.scalar.activation(lin_raw[:], t_lin[piece][:], IDENTITY, bias=b1_lin1[:])
 
-            y = psum.tile([P, PIECE], F32, name="y")
-            nc.tensor.matmul(y[:], w2_sb[:], h[:])
+            lin1 = work.tile([P, PIECE], F32, name="lin1")
+            nc.vector.tensor_scalar(
+                lin1[:], lin_raw[:], LIMIT + 1.0, -LIMIT + 1.0, MIN, MAX
+            )
+            h.append(work.tile([P, PIECE], BF16, name="h"))
+            nc.vector.scalar_tensor_tensor(
+                h[piece][:], swish[:], swish_cap[:], lin1[:], MIN, MULT
+            )
+
+        for piece in range(PIECES):
+            columns = slice(piece * PIECE, (piece + 1) * PIECE)
+            y = psum.tile([P, PIECE], F32, name="y", tag="bank")
+            nc.tensor.matmul(y[:], w2_sb[:], h[piece][:])
             scaled = work.tile([P, PIECE], F32, name="scaled")
             nc.vector.scalar_tensor_tensor(
                 scaled[:], y[:], b2_sb[:], routing[:, columns], ADD, MULT

@@ -8,6 +8,7 @@ PIECES = ROUTED // PIECE
 OFFSET_COLUMNS = PIECE // 16
 PSUM_BANKS = 8
 LIMIT = 7.0
+WARM_UP_MATMULS = 6
 
 FLOPS = 2 * P * (2 * P) * ROUTED + 2 * P * P * ROUTED
 
@@ -23,7 +24,7 @@ def tile_moemlpfused_kernel(tc, x, w1, b1, w2, b2, ew, offs, out):
     with (
         tc.tile_pool(name="held", bufs=1) as held,
         tc.tile_pool(name="work", bufs=PIECES) as work,
-        tc.psum_pool(name="psum", bufs=PSUM_BANKS) as psum,
+        tc.psum_pool(name="psum", bufs=1) as psum,
     ):
         offsets = held.tile([P, ROUTED // 16], U16, name="offsets")
         tokens = held.tile([P, TOKENS], BF16, name="tokens")
@@ -36,37 +37,41 @@ def tile_moemlpfused_kernel(tc, x, w1, b1, w2, b2, ew, offs, out):
         routing = held.tile([P, ROUTED], F32, name="routing")
         limit = held.tile([P, 1], F32, name="limit")
         swish_cap = held.tile([P, 1], F32, name="swish_cap")
+        idle_food = held.tile([P, PIECE], BF16, name="idle_food")
+        banks = [psum.tile([P, PIECE], F32, name=f"bank{b}") for b in range(PSUM_BANKS)]
 
-        nc.sync.dma_start(offsets[:], offs)
         nc.scalar.dma_start(tokens[:], x)
-        nc.gpsimd.dma_start(w1_sb[:], w1)
+        nc.sync.dma_start(offsets[:], offs)
+        nc.sync.dma_start(w1_sb[:], w1)
+        nc.sync.dma_start(b1_lin[:], b1[P : 2 * P, :])
         nc.sync.dma_start(b1_gate[:], b1[0:P, :])
-        nc.gpsimd.dma_start(b1_lin[:], b1[P : 2 * P, :])
-        nc.scalar.dma_start(routing[:], ew.broadcast_to([P, ROUTED]))
-        nc.gpsimd.dma_start(w2_sb[:], w2)
         nc.sync.dma_start(b2_sb[:], b2)
+        nc.scalar.dma_start(w2_sb[:], w2)
+        nc.scalar.dma_start(routing[:], ew.broadcast_to([P, ROUTED]))
+
+        nc.vector.memset(idle_food[:], 0.0)
+        for repeat in range(WARM_UP_MATMULS):
+            nc.tensor.matmul(banks[0][:], idle_food[:, 0:P], idle_food[:])
 
         nc.vector.memset(limit[:], LIMIT)
         nc.scalar.activation(swish_cap[:], limit[:], SWISH)
 
         nc.vector.tensor_scalar_add(b1_lin1[:], b1_lin[:], 1.0)
 
-        t_gate, t_lin = [], []
         for piece in range(PIECES):
             picked = tokens[:].indirect(
                 offsets[:, piece * OFFSET_COLUMNS : (piece + 1) * OFFSET_COLUMNS]
             )
-            t_gate.append(psum.tile([P, PIECE], F32, name=f"t_gate{piece}", tag="bank"))
-            t_lin.append(psum.tile([P, PIECE], F32, name=f"t_lin{piece}", tag="bank"))
-            nc.tensor.matmul(t_gate[piece][:], w1_sb[:, 0:P], picked)
-            nc.tensor.matmul(t_lin[piece][:], w1_sb[:, P : 2 * P], picked)
+            nc.tensor.matmul(banks[2 * piece][:], w1_sb[:, P : 2 * P], picked)
+            nc.tensor.matmul(banks[2 * piece + 1][:], w1_sb[:, 0:P], picked)
 
         h = []
         for piece in range(PIECES):
-            swish = work.tile([P, PIECE], F32, name="swish")
-            nc.scalar.activation(swish[:], t_gate[piece][:], SWISH, bias=b1_gate[:])
+            t_lin, t_gate = banks[2 * piece], banks[2 * piece + 1]
             lin_raw = work.tile([P, PIECE], F32, name="lin_raw")
-            nc.scalar.activation(lin_raw[:], t_lin[piece][:], IDENTITY, bias=b1_lin1[:])
+            nc.scalar.activation(lin_raw[:], t_lin[:], IDENTITY, bias=b1_lin1[:])
+            swish = work.tile([P, PIECE], F32, name="swish")
+            nc.scalar.activation(swish[:], t_gate[:], SWISH, bias=b1_gate[:])
 
             lin1 = work.tile([P, PIECE], F32, name="lin1")
             nc.vector.tensor_scalar(
@@ -79,10 +84,11 @@ def tile_moemlpfused_kernel(tc, x, w1, b1, w2, b2, ew, offs, out):
 
         for piece in range(PIECES):
             columns = slice(piece * PIECE, (piece + 1) * PIECE)
-            y = psum.tile([P, PIECE], F32, name="y", tag="bank")
+            y = banks[PSUM_BANKS - 1 - piece]
             nc.tensor.matmul(y[:], w2_sb[:], h[piece][:])
             scaled = work.tile([P, PIECE], F32, name="scaled")
             nc.vector.scalar_tensor_tensor(
                 scaled[:], y[:], b2_sb[:], routing[:, columns], ADD, MULT
             )
-            nc.sync.dma_start(out[:, columns], scaled[:])
+            store_queue = nc.sync if piece % 2 == 0 else nc.scalar
+            store_queue.dma_start(out[:, columns], scaled[:])

@@ -7,8 +7,9 @@ PIECE = 512
 PIECES = ROUTED // PIECE
 OFFSET_COLUMNS = PIECE // 16
 PSUM_BANKS = 8
+SHARED_PIECE = 1
 LIMIT = 7.0
-WARM_UP_MATMULS = 6
+WARM_UP_MATMULS = 10
 
 FLOPS = 2 * P * (2 * P) * ROUTED + 2 * P * P * ROUTED
 
@@ -84,11 +85,16 @@ def tile_moemlpfused_kernel(tc, x, w1, b1, w2, b2, ew, offs, out):
 
         for piece in range(PIECES):
             columns = slice(piece * PIECE, (piece + 1) * PIECE)
-            y = banks[PSUM_BANKS - 1 - piece]
+            y = banks[2 * (PIECES - 1 - piece // 2) + piece % 2]
             nc.tensor.matmul(y[:], w2_sb[:], h[piece][:])
             scaled = work.tile([P, PIECE], F32, name="scaled")
-            nc.vector.scalar_tensor_tensor(
-                scaled[:], y[:], b2_sb[:], routing[:, columns], ADD, MULT
-            )
+            if piece == SHARED_PIECE:
+                biased = held.tile([P, PIECE], F32, name="biased")
+                nc.scalar.activation(biased[:], y[:], IDENTITY, bias=b2_sb[:])
+                nc.gpsimd.tensor_tensor(scaled[:], biased[:], routing[:, columns], MULT)
+            else:
+                nc.vector.scalar_tensor_tensor(
+                    scaled[:], y[:], b2_sb[:], routing[:, columns], ADD, MULT
+                )
             store_queue = nc.sync if piece % 2 == 0 else nc.scalar
             store_queue.dma_start(out[:, columns], scaled[:])

@@ -7,9 +7,8 @@ PIECE = 512
 PIECES = ROUTED // PIECE
 OFFSET_COLUMNS = PIECE // 16
 PSUM_BANKS = 8
-SHARED_PIECE = 1
 LIMIT = 7.0
-WARM_UP_MATMULS = 10
+WARM_UP_MATMULS = 6
 
 FLOPS = 2 * P * (2 * P) * ROUTED + 2 * P * P * ROUTED
 
@@ -88,13 +87,8 @@ def tile_moemlpfused_kernel(tc, x, w1, b1, w2, b2, ew, offs, out):
             y = banks[2 * (PIECES - 1 - piece // 2) + piece % 2]
             nc.tensor.matmul(y[:], w2_sb[:], h[piece][:])
             scaled = work.tile([P, PIECE], F32, name="scaled")
-            if piece == SHARED_PIECE:
-                biased = held.tile([P, PIECE], F32, name="biased")
-                nc.scalar.activation(biased[:], y[:], IDENTITY, bias=b2_sb[:])
-                nc.gpsimd.tensor_tensor(scaled[:], biased[:], routing[:, columns], MULT)
-            else:
-                nc.vector.scalar_tensor_tensor(
-                    scaled[:], y[:], b2_sb[:], routing[:, columns], ADD, MULT
-                )
+            nc.vector.scalar_tensor_tensor(
+                scaled[:], y[:], b2_sb[:], routing[:, columns], ADD, MULT
+            )
             store_queue = nc.sync if piece % 2 == 0 else nc.scalar
             store_queue.dma_start(out[:, columns], scaled[:])

@@ -83,12 +83,16 @@ def tile_moemlpfused_kernel(tc, x, w1, b1, w2, b2, ew, offs, out):
             )
 
         for piece in range(PIECES):
-            columns = slice(piece * PIECE, (piece + 1) * PIECE)
             y = banks[2 * (PIECES - 1 - piece // 2) + piece % 2]
             nc.tensor.matmul(y[:], w2_sb[:], h[piece][:])
             scaled = work.tile([P, PIECE], F32, name="scaled")
-            nc.vector.scalar_tensor_tensor(
-                scaled[:], y[:], b2_sb[:], routing[:, columns], ADD, MULT
-            )
-            store_queue = nc.sync if piece % 2 == 0 else nc.scalar
-            store_queue.dma_start(out[:, columns], scaled[:])
+            parts = 2 if piece == PIECES - 1 else 1
+            width = PIECE // parts
+            for part in range(parts):
+                local = slice(part * width, (part + 1) * width)
+                columns = slice(piece * PIECE + part * width, piece * PIECE + (part + 1) * width)
+                nc.vector.scalar_tensor_tensor(
+                    scaled[:, local], y[:, local], b2_sb[:], routing[:, columns], ADD, MULT
+                )
+                store_queue = nc.sync if (piece + part) % 2 == 0 else nc.scalar
+                store_queue.dma_start(out[:, columns], scaled[:, local])

@@ -30,8 +30,7 @@ def tile_moemlpfused_kernel(tc, x, w1, b1, w2, b2, ew, offs, out):
         tokens = held.tile([P, TOKENS], BF16, name="tokens")
         w1_sb = held.tile([P, 2 * P], BF16, name="w1_sb")
         w2_sb = held.tile([P, P], BF16, name="w2_sb")
-        b1_gate = held.tile([P, 1], F32, name="b1_gate")
-        b1_lin = held.tile([P, 1], F32, name="b1_lin")
+        b1_sb = held.tile([P, 2], F32, name="b1_sb")
         b1_lin1 = held.tile([P, 1], F32, name="b1_lin1")
         b2_sb = held.tile([P, 1], F32, name="b2_sb")
         routing = held.tile([P, ROUTED], F32, name="routing")
@@ -43,10 +42,9 @@ def tile_moemlpfused_kernel(tc, x, w1, b1, w2, b2, ew, offs, out):
         nc.scalar.dma_start(tokens[:], x)
         nc.sync.dma_start(offsets[:], offs)
         nc.sync.dma_start(w1_sb[:], w1)
-        nc.sync.dma_start(b1_lin[:], b1[P : 2 * P, :])
-        nc.sync.dma_start(b1_gate[:], b1[0:P, :])
-        nc.sync.dma_start(b2_sb[:], b2)
+        nc.scalar.dma_start(b1_sb[:], b1.rearrange("(half p) one -> p (half one)", p=P))
         nc.scalar.dma_start(w2_sb[:], w2)
+        nc.scalar.dma_start(b2_sb[:], b2)
         nc.scalar.dma_start(routing[:], ew.broadcast_to([P, ROUTED]))
 
         nc.vector.memset(idle_food[:], 0.0)
@@ -56,7 +54,7 @@ def tile_moemlpfused_kernel(tc, x, w1, b1, w2, b2, ew, offs, out):
         nc.vector.memset(limit[:], LIMIT)
         nc.scalar.activation(swish_cap[:], limit[:], SWISH)
 
-        nc.vector.tensor_scalar_add(b1_lin1[:], b1_lin[:], 1.0)
+        nc.vector.tensor_scalar_add(b1_lin1[:], b1_sb[:, 1:2], 1.0)
 
         for piece in range(PIECES):
             picked = tokens[:].indirect(
@@ -71,7 +69,7 @@ def tile_moemlpfused_kernel(tc, x, w1, b1, w2, b2, ew, offs, out):
             lin_raw = work.tile([P, PIECE], F32, name="lin_raw")
             nc.scalar.activation(lin_raw[:], t_lin[:], IDENTITY, bias=b1_lin1[:])
             swish = work.tile([P, PIECE], F32, name="swish")
-            nc.scalar.activation(swish[:], t_gate[:], SWISH, bias=b1_gate[:])
+            nc.scalar.activation(swish[:], t_gate[:], SWISH, bias=b1_sb[:, 0:1])
 
             lin1 = work.tile([P, PIECE], F32, name="lin1")
             nc.vector.tensor_scalar(

@@ -8,7 +8,6 @@ PIECES = ROUTED // PIECE
 OFFSET_COLUMNS = PIECE // 16
 PSUM_BANKS = 8
 LIMIT = 7.0
-WARM_UP_MATMULS = 6
 
 FLOPS = 2 * P * (2 * P) * ROUTED + 2 * P * P * ROUTED
 
@@ -36,7 +35,6 @@ def tile_moemlpfused_kernel(tc, x, w1, b1, w2, b2, ew, offs, out):
         routing = held.tile([P, ROUTED], F32, name="routing")
         limit = held.tile([P, 1], F32, name="limit")
         swish_cap = held.tile([P, 1], F32, name="swish_cap")
-        idle_food = held.tile([P, PIECE], BF16, name="idle_food")
         banks = [psum.tile([P, PIECE], F32, name=f"bank{b}") for b in range(PSUM_BANKS)]
 
         nc.scalar.dma_start(tokens[:], x)
@@ -46,10 +44,6 @@ def tile_moemlpfused_kernel(tc, x, w1, b1, w2, b2, ew, offs, out):
         nc.scalar.dma_start(w2_sb[:], w2)
         nc.scalar.dma_start(b2_sb[:], b2)
         nc.scalar.dma_start(routing[:], ew.broadcast_to([P, ROUTED]))
-
-        nc.vector.memset(idle_food[:], 0.0)
-        for repeat in range(WARM_UP_MATMULS):
-            nc.tensor.matmul(banks[0][:], idle_food[:, 0:P], idle_food[:])
 
         nc.vector.memset(limit[:], LIMIT)
         nc.scalar.activation(swish_cap[:], limit[:], SWISH)

@@ -62,17 +62,22 @@ def tile_moemlpfused_kernel(tc, x, w1, b1, w2, b2, ew, offs, out):
             t_lin, t_gate = banks[2 * piece], banks[2 * piece + 1]
             lin_raw = work.tile([P, PIECE], F32, name="lin_raw")
             nc.scalar.activation(lin_raw[:], t_lin[:], IDENTITY, bias=b1_lin1[:])
-            swish = work.tile([P, PIECE], F32, name="swish")
-            nc.scalar.activation(swish[:], t_gate[:], SWISH, bias=b1_sb[:, 0:1])
-
             lin1 = work.tile([P, PIECE], F32, name="lin1")
             nc.vector.tensor_scalar(
                 lin1[:], lin_raw[:], LIMIT + 1.0, -LIMIT + 1.0, MIN, MAX
             )
+            swish = work.tile([P, PIECE], F32, name="swish")
             h.append(work.tile([P, PIECE], BF16, name="h"))
-            nc.vector.scalar_tensor_tensor(
-                h[piece][:], swish[:], swish_cap[:], lin1[:], MIN, MULT
-            )
+            parts = 2 if piece == PIECES - 1 else 1
+            width = PIECE // parts
+            for part in range(parts):
+                local = slice(part * width, (part + 1) * width)
+                nc.scalar.activation(
+                    swish[:, local], t_gate[:, local], SWISH, bias=b1_sb[:, 0:1]
+                )
+                nc.vector.scalar_tensor_tensor(
+                    h[piece][:, local], swish[:, local], swish_cap[:], lin1[:, local], MIN, MULT
+                )
 
         for piece in range(PIECES):
             y = banks[2 * (PIECES - 1 - piece // 2) + piece % 2]

import concourse.mybir as mybir

P = 128
TOKENS = 4096
ROUTED = 2048
PIECE = 512
PIECES = ROUTED // PIECE
OFFSET_COLUMNS = PIECE // 16
PSUM_BANKS = 8
LIMIT = 7.0

FLOPS = 2 * P * (2 * P) * ROUTED + 2 * P * P * ROUTED

BF16, F32, U16 = mybir.dt.bfloat16, mybir.dt.float32, mybir.dt.uint16
ADD, MULT = mybir.AluOpType.add, mybir.AluOpType.mult
MIN, MAX = mybir.AluOpType.min, mybir.AluOpType.max
SWISH = mybir.ActivationFunctionType.Gelu_apprx_sigmoid
IDENTITY = mybir.ActivationFunctionType.Identity


def tile_moemlpfused_kernel(tc, x, w1, b1, w2, b2, ew, offs, out):
    nc = tc.nc
    with (
        tc.tile_pool(name="held", bufs=1) as held,
        tc.tile_pool(name="work", bufs=PIECES) as work,
        tc.psum_pool(name="psum", bufs=1) as psum,
    ):
        offsets = held.tile([P, ROUTED // 16], U16, name="offsets")
        tokens = held.tile([P, TOKENS], BF16, name="tokens")
        w1_sb = held.tile([P, 2 * P], BF16, name="w1_sb")
        w2_sb = held.tile([P, P], BF16, name="w2_sb")
        b1_sb = held.tile([P, 2], F32, name="b1_sb")
        b1_lin1 = held.tile([P, 1], F32, name="b1_lin1")
        b2_sb = held.tile([P, 1], F32, name="b2_sb")
        routing = held.tile([P, ROUTED], F32, name="routing")
        limit = held.tile([P, 1], F32, name="limit")
        swish_cap = held.tile([P, 1], F32, name="swish_cap")
        banks = [psum.tile([P, PIECE], F32, name=f"bank{b}") for b in range(PSUM_BANKS)]

        nc.scalar.dma_start(tokens[:], x)
        nc.sync.dma_start(offsets[:], offs)
        nc.sync.dma_start(w1_sb[:], w1)
        nc.scalar.dma_start(b1_sb[:], b1.rearrange("(half p) one -> p (half one)", p=P))
        nc.scalar.dma_start(w2_sb[:], w2)
        nc.scalar.dma_start(b2_sb[:], b2)
        nc.scalar.dma_start(routing[:], ew.broadcast_to([P, ROUTED]))

        nc.vector.memset(limit[:], LIMIT)
        nc.scalar.activation(swish_cap[:], limit[:], SWISH)

        nc.vector.tensor_scalar_add(b1_lin1[:], b1_sb[:, 1:2], 1.0)

        for piece in range(PIECES):
            picked = tokens[:].indirect(
                offsets[:, piece * OFFSET_COLUMNS : (piece + 1) * OFFSET_COLUMNS]
            )
            nc.tensor.matmul(banks[2 * piece][:], w1_sb[:, P : 2 * P], picked)
            nc.tensor.matmul(banks[2 * piece + 1][:], w1_sb[:, 0:P], picked)

        h = []
        for piece in range(PIECES):
            t_lin, t_gate = banks[2 * piece], banks[2 * piece + 1]
            lin_raw = work.tile([P, PIECE], F32, name="lin_raw")
            nc.scalar.activation(lin_raw[:], t_lin[:], IDENTITY, bias=b1_lin1[:])
            lin1 = work.tile([P, PIECE], F32, name="lin1")
            nc.vector.tensor_scalar(
                lin1[:], lin_raw[:], LIMIT + 1.0, -LIMIT + 1.0, MIN, MAX
            )
            swish = work.tile([P, PIECE], F32, name="swish")
            h.append(work.tile([P, PIECE], BF16, name="h"))
            parts = 2 if piece == PIECES - 1 else 1
            width = PIECE // parts
            for part in range(parts):
                local = slice(part * width, (part + 1) * width)
                nc.scalar.activation(
                    swish[:, local], t_gate[:, local], SWISH, bias=b1_sb[:, 0:1]
                )
                nc.vector.scalar_tensor_tensor(
                    h[piece][:, local], swish[:, local], swish_cap[:], lin1[:, local], MIN, MULT
                )

        for piece in range(PIECES):
            y = banks[2 * (PIECES - 1 - piece // 2) + piece % 2]
            nc.tensor.matmul(y[:], w2_sb[:], h[piece][:])
            scaled = work.tile([P, PIECE], F32, name="scaled")
            parts = 2 if piece == PIECES - 1 else 1
            width = PIECE // parts
            for part in range(parts):
                local = slice(part * width, (part + 1) * width)
                columns = slice(piece * PIECE + part * width, piece * PIECE + (part + 1) * width)
                nc.vector.scalar_tensor_tensor(
                    scaled[:, local], y[:, local], b2_sb[:], routing[:, columns], ADD, MULT
                )
                store_queue = nc.sync if (piece + part) % 2 == 0 else nc.scalar
                store_queue.dma_start(out[:, columns], scaled[:, local])
